import numpy as np
import ml_dtypes


def mxq(x, axis, fmt="e4m3"):
    dtype, down = {"e4m3": (ml_dtypes.float8_e4m3fn, 7), "e5m2": (ml_dtypes.float8_e5m2, 14)}[fmt]
    v = np.moveaxis(np.asarray(x, np.float32).astype(ml_dtypes.bfloat16).astype(np.float64), axis, -1)
    blocks = v.reshape(v.shape[:-1] + (-1, 32))
    amax = np.abs(blocks).max(-1, keepdims=True)
    byte = np.maximum(np.where(amax > 0, np.frexp(amax)[1] - 1 + 127, 0) - down, 1)
    scale = np.exp2(byte - 127.0)
    codes = (blocks / scale).astype(np.float32).astype(dtype).astype(np.float64)
    return np.moveaxis((codes * scale).reshape(v.shape), -1, axis)


WIDE = False


def mx_kscale(k):
    if not WIDE:
        return np.ones(k)
    levels = np.array([10, -10, 5, -5, 0])
    if k % 512:
        return np.exp2(np.random.permutation(np.resize(levels, k // 32))).repeat(32)
    a = np.empty((k // 512, 16))
    for p in range(k // 512):
        a[p, :8] = np.random.permutation(np.resize(levels, 8))
        for g in range(8):
            far = levels[np.abs(levels - a[p, g]) >= 10]
            a[p, g + 8] = far[np.random.randint(len(far))]
    return np.exp2(a.ravel()).repeat(32)


BF16 = ml_dtypes.bfloat16


def bf(x):
    return np.asarray(x, np.float32).astype(BF16)


def f64(x):
    return np.asarray(x).astype(np.float64)


E2M1 = np.array([0.0, 0.5, 1.0, 1.5, 2.0, 3.0, 4.0, 6.0, -0.0, -0.5, -1.0, -1.5, -2.0, -3.0, -4.0, -6.0])


def pack_weight(w, fmt):
    k, n = w.shape
    w = f64(bf(w)).reshape(k // 32, 32, n)
    amax = np.abs(w).max(1)
    if fmt == "e4m3":
        byte = np.frexp(amax)[1] - 1 + 127 - 7
    else:
        mant, ex = np.frexp(amax / 6.0)
        byte = np.where(mant > 0.5, ex, ex - 1) + 127
    byte = np.clip(np.where(amax > 0, byte, 1), 1, 254)
    scaled = (w * np.exp2(127.0 - byte)[:, None, :]).reshape(k, n).astype(np.float32)
    by_word = np.ascontiguousarray(scaled.reshape(k // 512, 128, 4, n).transpose(0, 1, 3, 2))
    if fmt == "e4m3":
        words = by_word.astype(ml_dtypes.float8_e4m3fn).view(np.uint8)
    else:
        c = by_word.astype(ml_dtypes.float4_e2m1fn).view(np.uint8) & 0xF
        words = c[..., 0::2] | (c[..., 1::2] << 4)
    return np.ascontiguousarray(words), np.ascontiguousarray(byte.astype(np.uint8).reshape(k // 512, 16, n))


def unpack_weight(words, scales, fmt):
    g, p, n, _ = words.shape
    if fmt == "e4m3":
        vals = np.ascontiguousarray(words).view(ml_dtypes.float8_e4m3fn).astype(np.float64)
    else:
        nib = np.empty((g, p, n, 4), np.uint8)
        nib[..., 0::2] = words & 0xF
        nib[..., 1::2] = words >> 4
        vals = E2M1[nib]
    vals = vals * np.repeat(np.exp2(scales.astype(np.float64) - 127.0), 8, axis=1)[..., None]
    return vals.transpose(0, 1, 3, 2).reshape(g * 512, n)
def pack4(w):
    words, scales = pack_weight(w, "e2m1")
    return words.reshape(words.shape[0], 128, -1), scales


def unpack4(words, scales):
    return unpack_weight(words.reshape(words.shape[0], 128, -1, 2), scales, "e2m1")


B, A, C, D, K0, K1, K2 = 2, 128, 64, 512, 512, 128, 256
D2 = D + D
NEG_SLOPE = 0.01


def leaky(v):
    return np.where(v >= 0, v, NEG_SLOPE * v)


def draw0():
    s, t = mx_kscale(D), mx_kscale(K0)
    ss = np.concatenate([s, s])
    sent_a = bf(np.random.standard_normal((B, A, D)) * s)
    sent_b = bf(np.random.standard_normal((B, C, D)) * s)
    W1_words, W1_scales = pack4(np.random.standard_normal((D2, K0)) / np.sqrt(D2) / ss[:, None] * t)
    b1 = bf((np.random.standard_normal(K0) * 0.5 - 0.5) * t)
    W2_words, W2_scales = pack4(np.random.standard_normal((K0, K1)) * 2.0 / np.sqrt(K0) / t[:, None])
    b2 = bf(np.random.standard_normal(K1) * 0.5 - 0.5)
    return {"sent_a": sent_a,
            "sent_b": sent_b,
            "W1_words": W1_words,
            "W1_scales": W1_scales,
            "b1": b1,
            "W2_words": W2_words,
            "W2_scales": W2_scales,
            "b2": b2}


def core(sent_a, sent_b, W1_words, W1_scales, b1, W2_words, W2_scales, b2):
    w1 = unpack4(W1_words, W1_scales)
    a_part = mxq(f64(sent_a), 2, "e4m3") @ w1[:D]
    b_part = mxq(f64(sent_b), 2, "e4m3") @ w1[D:]
    h = leaky(a_part[:, :, None, :] + b_part[:, None, :, :] + f64(b1))
    return leaky((mxq(h, 3, "e4m3") @ unpack4(W2_words, W2_scales)) + f64(b2))


def e4m3fn_bytes(y):
    return np.clip(np.asarray(y, np.float64), -448.0, 448.0).astype(np.float32).astype(ml_dtypes.float8_e4m3fn).view(np.uint8)


def e4m3fn_values(b):
    return np.asarray(b, np.uint8).view(ml_dtypes.float8_e4m3fn).astype(np.float64)


def setup_inputs():
    d = draw0()
    x0 = np.asarray(d['sent_a']).astype(np.float64)
    s = (np.max(np.abs(x0), axis=(0, 1), keepdims=True) / 448.0).astype(np.float32)
    out = {}
    for k, v in d.items():
        if k == 'sent_a':
            out['sent_a_bytes'] = e4m3fn_bytes(x0 / s.astype(np.float64))
            out['sent_a_scale'] = s
        else:
            out[k] = v
    return out


def reference(sent_a_bytes, sent_a_scale, sent_b, W1_words, W1_scales, b1, W2_words, W2_scales, b2):
    return core(e4m3fn_values(sent_a_bytes) * sent_a_scale.astype(np.float64), sent_b, W1_words, W1_scales, b1, W2_words, W2_scales, b2)

@@ -1,0 +1,316 @@
+from contextlib import ExitStack
+
+import concourse.mybir as mybir
+from concourse.masks import make_identity
+
+F32 = mybir.dt.float32
+BF16 = mybir.dt.bfloat16
+I32 = mybir.dt.int32
+U32 = mybir.dt.uint32
+U8 = mybir.dt.uint8
+FP8 = mybir.dt.float8_e4m3fn
+FP8X4 = mybir.dt.float8_e4m3fn_x4
+FP4X4 = mybir.dt.float4_e2m1fn_x4
+ALU = mybir.AluOpType
+COPY = mybir.ActivationFunctionType.Copy
+
+P = 128
+NB, NI, NJ, D, K0, K1 = 2, 128, 64, 512, 512, 128
+FLOPS = 2 * (NB * (NI + NJ) * D * K0 + NB * NI * NJ * K0 * K1)
+SLOPE = 0.01
+R = 8
+W = 8
+Z = 16
+QUAD = 4
+TWO_READ = (0,)
+
+
+def tile_matchmatrix_pa_t_w4_kernel(
+    tc, sent_a_bytes, sent_a_scale, sent_b, w1_words, w1_scales, b1, w2_words, w2_scales, b2, out
+):
+    nc = tc.nc
+    with ExitStack() as ctx:
+        keep = ctx.enter_context(tc.tile_pool(name="keep", bufs=1))
+        work = ctx.enter_context(tc.tile_pool(name="work", bufs=3))
+        xps = ctx.enter_context(tc.psum_pool(name="xps", bufs=6))
+        yps = ctx.enter_context(tc.psum_pool(name="yps", bufs=2))
+        ctx.enter_context(tc.manual_schedule())
+
+        b_raw = keep.tile([P, D], BF16, align_bytes=64)
+        nc.sync.dma_start(out=b_raw[:], in_=sent_b.rearrange("n j k -> (n j) k"))
+        a_bytes = keep.tile([P, NB, D], U8, align_bytes=64)
+        nc.sync.dma_start(out=a_bytes[:], in_=sent_a_bytes.rearrange("n i k -> i n k"))
+        a_scale = keep.tile([P, D], F32)
+        nc.scalar.dma_start(out=a_scale[:], in_=sent_a_scale.rearrange("x y k -> (x y k)").partition_broadcast(P))
+        w1 = keep.tile([P, 2, 2 * K0], U8, align_bytes=64)
+        nc.sync.dma_start(out=w1[:, 0, :].bitcast(I32), in_=w1_words[0].bitcast(I32))
+        nc.sync.dma_start(out=w1[:, 1, :].bitcast(I32), in_=w1_words[1].bitcast(I32))
+        b1_all = keep.tile([P, K0], BF16)
+        nc.scalar.dma_start(out=b1_all[:], in_=b1.partition_broadcast(P))
+        b2_all = keep.tile([P, K1], BF16)
+        nc.scalar.dma_start(out=b2_all[:], in_=b2.partition_broadcast(P))
+
+        w1_sc = keep.tile([P, 2, K0], U8, align_bytes=64)
+        w2_sc = keep.tile([P, K1], U8, align_bytes=64)
+        b_scales = keep.tile([P, P], U8, align_bytes=64)
+        nc.vector.memset(w1_sc[:].rearrange("p g n -> p (g n)").bitcast(I32), 0)
+        nc.vector.memset(b_scales[:].bitcast(I32), 0)
+        nc.vector.memset(w2_sc[:].bitcast(I32), 0)
+        for q in range(4):
+            nc.sync.dma_start(
+                out=w1_sc[32 * q : 32 * q + 4, :, :].bitcast(I32),
+                in_=w1_scales[:, 4 * q : 4 * q + 4, :].rearrange("g q n -> q g n").bitcast(I32),
+            )
+        w2 = keep.tile([P, 2 * K1], U8, align_bytes=64)
+        nc.sync.dma_start(out=w2[:].bitcast(I32), in_=w2_words[0].bitcast(I32))
+        for q in range(4):
+            nc.sync.dma_start(
+                out=w2_sc[32 * q : 32 * q + 4, :].bitcast(I32),
+                in_=w2_scales[0, 4 * q : 4 * q + 4, :].bitcast(I32),
+            )
+
+        ident = keep.tile([P, P], F32)
+        make_identity(nc, ident[:])
+        shifts = keep.tile([P, 2 * W, Z], F32)
+        for half in range(2):
+            nc.vector.tensor_copy(
+                out=shifts[:, half * W : (half + 1) * W, :], in_=ident[:].rearrange("q (z w) -> q w z", w=W)
+            )
+
+        def turn(raw):
+            words = raw.bitcast(F32)
+            xt = xps.tile([P, 2, P], F32, name="xt", tag="x")
+            for u in range(2):
+                nc.tensor.transpose(xt[:, u, :], words[:, u : 2 * P : 2], ident[:])
+            return xt
+
+        def widen(n):
+            a_raw = keep.tile([P, D], BF16, align_bytes=64, name=f"a_raw{n}")
+            nc.vector.tensor_tensor(out=a_raw[:], in0=a_bytes[:, n, :].bitcast(FP8), in1=a_scale[:], op=ALU.mult)
+            return a_raw
+
+        b_grouped = keep.tile([P, P, 4], BF16, align_bytes=64)
+        b_codes = keep.tile([P, P], U32, align_bytes=64)
+        xt_b = turn(b_raw[:])
+        a_raw0 = widen(0)
+        for n in range(NB):
+            nc.vector.tensor_copy(
+                out=b_grouped[:, n * NJ : (n + 1) * NJ, :]
+                .rearrange("p c t -> p (c t)")
+                .bitcast(F32)
+                .rearrange("p (r w u) -> p r w u", r=R, w=W),
+                in_=xt_b[:, :, n * NJ : (n + 1) * NJ].rearrange("p u (w r) -> p r w u", r=R),
+            )
+        nc.vector.quantize_mx(
+            out=b_codes[:].bitcast(FP8X4), scales=b_scales[:], in_=b_grouped[:].rearrange("p c t -> p (c t)")
+        )
+
+        def group_a(n, xt):
+            a_grouped = keep.tile([P, P, 4], BF16, align_bytes=64, name=f"a_grouped{n}")
+            nc.scalar.copy(
+                out=a_grouped[:].rearrange("p c t -> p (c t)").bitcast(F32).rearrange("p (c u) -> p c u", u=2),
+                in_=xt[:].rearrange("p u c -> p c u"),
+            )
+            return a_grouped
+
+        def quantize_a(n, a_grouped):
+            a_codes = keep.tile([P, P], U32, align_bytes=64, name=f"a_codes{n}")
+            a_scales = keep.tile([P, P], U8, align_bytes=64, name=f"a_scales{n}")
+            nc.vector.quantize_mx(
+                out=a_codes[:].bitcast(FP8X4), scales=a_scales[:], in_=a_grouped[:].rearrange("p c t -> p (c t)")
+            )
+            return a_codes, a_scales
+
+        rep_codes = keep.tile([P, NB, R, Z, W], U32, align_bytes=64)
+        rep_scales = keep.tile([P, NB, R, Z, W], U8, align_bytes=64)
+
+        def repeat_b(n):
+            cols = slice(n * NJ, (n + 1) * NJ)
+            nc.vector.tensor_copy(
+                out=rep_codes[:, n].rearrange("p r z w -> p (r z w)").bitcast(I32).rearrange("p (r z w) -> p r z w", r=R, z=Z),
+                in_=b_codes[:, cols].bitcast(I32).rearrange("p (r w) -> p r w", r=R).unsqueeze(2).to_broadcast([P, R, Z, W]),
+            )
+            nc.vector.tensor_copy(
+                out=rep_scales[:, n].rearrange("p r z w -> p (r z w)").bitcast(I32).rearrange("p (r z w) -> p r z w", r=R, z=Z),
+                in_=b_scales[:, cols]
+                .bitcast(I32)
+                .rearrange("p (r w) -> p r w", r=R)
+                .unsqueeze(2)
+                .to_broadcast([P, R, Z, W // 4]),
+            )
+
+        a_part = keep.tile([P, NB, 4, P], F32)
+        b_part = keep.tile([P, NB, R, 4, P], F32)
+
+        def a_layer(n, a_codes, a_scales):
+            pa = xps.tile([P, K0], F32, name="pa", tag="x")
+            nc.tensor.matmul_mx(
+                out=pa[:],
+                lhsT=a_codes[:].bitcast(FP8X4),
+                lhsT_scale=a_scales[:],
+                rhs=w1[:, 0, :].bitcast(FP4X4),
+                rhs_scale=w1_sc[:, 0, :],
+                start=True,
+                stop=True,
+            )
+            nc.vector.tensor_tensor(
+                out=a_part[:, n],
+                in0=pa[:].rearrange("i (m t) -> i t m", t=4),
+                in1=b1_all[:].rearrange("i (m t) -> i t m", t=4),
+                op=ALU.add,
+            )
+
+        def b_layer(n, r):
+            pb = xps.tile([P, K0], F32, name="pb", tag="x")
+            nc.tensor.matmul_mx(
+                out=pb[:],
+                lhsT=rep_codes[:, n, r].rearrange("p z w -> p (z w)").bitcast(FP8X4),
+                lhsT_scale=rep_scales[:, n, r].rearrange("p z w -> p (z w)"),
+                rhs=w1[:, 1, :].bitcast(FP4X4),
+                rhs_scale=w1_sc[:, 1, :],
+                start=True,
+                stop=True,
+            )
+            dst = b_part[:, n, r]
+            view = pb[:].rearrange("q (m t) -> q t m", t=4)
+            if r % 2 == 0:
+                nc.scalar.copy(out=dst, in_=view)
+            else:
+                nc.vector.tensor_copy(out=dst, in_=view)
+
+        xt_a0 = turn(a_raw0[:])
+        grouped0 = group_a(0, xt_a0)
+        repeat_b(0)
+        codes0, scales0 = quantize_a(0, grouped0)
+        a_layer(0, codes0, scales0)
+        for r in range(QUAD):
+            b_layer(0, r)
+
+        quads = [(n, s, h) for n in range(NB) for s in range(W) for h in range(2)]
+        live = {}
+        outs = {}
+
+        def sums(q):
+            n, s, half = quads[q]
+            picks = shifts[:].rearrange("q w z -> q (w z)")[:, s * Z : s * Z + P]
+            firsts = []
+            seconds = []
+            xs = []
+            for b in range(QUAD):
+                r = half * QUAD + b
+                x = xps.tile([P, 4, P], F32, name="x", tag="x")
+                for t in range(4):
+                    nc.tensor.matmul(
+                        x[:, t, :], lhsT=a_part[:, n, t, :], rhs=ident[:], is_transpose=True, start=True, stop=False
+                    )
+                    nc.tensor.matmul(
+                        x[:, t, :], lhsT=b_part[:, n, r, t, :], rhs=picks, is_transpose=True, start=False, stop=True
+                    )
+                first = work.tile([P, P, 4], BF16, name="first", tag="first", bufs=6)
+                nc.scalar.copy(out=first[:], in_=x[:].rearrange("m t c -> m c t"))
+                second = None
+                if b in TWO_READ:
+                    second = work.tile([P, P, 4], BF16, name="second", tag="second", bufs=4)
+                    nc.scalar.activation(out=second[:], in_=x[:].rearrange("m t c -> m c t"), func=COPY, scale=SLOPE)
+                xs.append(x)
+                firsts.append(first)
+                seconds.append(second)
+            hidden = work.tile([P, QUAD, P, 4], BF16, name="hidden", tag="hidden", align_bytes=64)
+            live[q] = (xs, firsts, seconds, hidden)
+
+        def leaky(q, b):
+            xs, firsts, seconds, hidden = live[q]
+            if seconds[b] is None:
+                nc.vector.scalar_tensor_tensor(
+                    out=hidden[:, b],
+                    in0=xs[b][:].rearrange("m t c -> m c t"),
+                    scalar=SLOPE,
+                    in1=firsts[b][:],
+                    op0=ALU.mult,
+                    op1=ALU.max,
+                )
+            else:
+                nc.vector.tensor_tensor(out=hidden[:, b], in0=firsts[b][:], in1=seconds[b][:], op=ALU.max)
+
+        def quantize(q):
+            hidden = live[q][3]
+            codes = work.tile([P, QUAD * P], U32, name="codes", tag="codes", align_bytes=64)
+            scales = work.tile([P, QUAD * P], U8, name="scales", tag="scales", align_bytes=64)
+            nc.vector.quantize_mx(
+                out=codes[:].bitcast(FP8X4), scales=scales[:], in_=hidden[:].rearrange("m b c t -> m (b c t)")
+            )
+            live[q] = (codes, scales)
+
+        def second_layer(q):
+            codes, scales = live[q]
+            y = yps.tile([P, QUAD, K1], F32, name="y", tag="y")
+            for b in range(QUAD):
+                cols = slice(b * P, (b + 1) * P)
+                nc.tensor.matmul_mx(
+                    out=y[:, b, :],
+                    lhsT=codes[:, cols].bitcast(FP8X4),
+                    lhsT_scale=scales[:, cols],
+                    rhs=w2[:].bitcast(FP4X4),
+                    rhs_scale=w2_sc[:],
+                    start=True,
+                    stop=True,
+                )
+            live[q] = y
+
+        def add_bias(q):
+            y = live[q]
+            z = work.tile([P, QUAD, K1], F32, name="z", tag="z")
+            nc.vector.tensor_tensor(
+                out=z[:], in0=y[:], in1=b2_all[:].unsqueeze(1).to_broadcast([P, QUAD, K1]), op=ALU.add
+            )
+            live[q] = z
+
+        def finish(q):
+            n, s, half = quads[q]
+            z = live.pop(q)
+            if half == 0:
+                outs[q // 2] = work.tile([P, R, K1], F32, name="o", tag="o")
+            o = outs[q // 2]
+            lift = work.tile([P, QUAD, K1], F32, name="lift", tag="lift", bufs=2)
+            nc.gpsimd.tensor_scalar(
+                out=lift[:], in0=z[:], scalar1=0.0, scalar2=SLOPE - 1.0, op0=ALU.min, op1=ALU.mult
+            )
+            nc.gpsimd.tensor_tensor(out=o[:, half * QUAD : (half + 1) * QUAD, :], in0=z[:], in1=lift[:], op=ALU.add)
+            if half == 1:
+                for w in range(W):
+                    j0 = R * ((w + s) % W)
+                    rows = slice(Z * w, Z * (w + 1))
+                    nc.sync.dma_start(out=out[n, rows, j0 : j0 + R, :], in_=o[rows, :, :])
+
+        last = len(quads)
+        state = {}
+        for q in range(last + 2):
+            if q < last:
+                sums(q)
+            if q < last:
+                leaky(q, 0)
+            if 1 <= q <= last:
+                quantize(q - 1)
+            if q >= 2:
+                add_bias(q - 2)
+            if q < last:
+                for b in range(1, QUAD):
+                    leaky(q, b)
+            if q >= 2:
+                finish(q - 2)
+            if 1 <= q <= last:
+                second_layer(q - 1)
+            if q == 0:
+                for r in range(QUAD, R):
+                    b_layer(0, r)
+            if q == 3:
+                state["raw"] = widen(1)
+            if q == 4:
+                state["grouped"] = group_a(1, turn(state["raw"][:]))
+                repeat_b(1)
+            if q == 5:
+                state["codes"] = quantize_a(1, state["grouped"])
+            if q == 6:
+                a_layer(1, state["codes"][0], state["codes"][1])
+            if 7 <= q < 7 + R:
+                b_layer(1, q - 7)

@@ -22,7 +22,7 @@ R = 8
 W = 8
 Z = 16
 QUAD = 4
-TWO_READ = (0,)
+TWO_READ = (0, 1)
 
 
 def tile_matchmatrix_pa_t_w4_kernel(
@@ -271,11 +271,9 @@ def tile_matchmatrix_pa_t_w4_kernel(
             if half == 0:
                 outs[q // 2] = work.tile([P, R, K1], F32, name="o", tag="o")
             o = outs[q // 2]
-            lift = work.tile([P, QUAD, K1], F32, name="lift", tag="lift", bufs=2)
-            nc.gpsimd.tensor_scalar(
-                out=lift[:], in0=z[:], scalar1=0.0, scalar2=SLOPE - 1.0, op0=ALU.min, op1=ALU.mult
+            nc.vector.scalar_tensor_tensor(
+                out=o[:, half * QUAD : (half + 1) * QUAD, :], in0=z[:], scalar=SLOPE, in1=z[:], op0=ALU.mult, op1=ALU.max
             )
-            nc.gpsimd.tensor_tensor(out=o[:, half * QUAD : (half + 1) * QUAD, :], in0=z[:], in1=lift[:], op=ALU.add)
             if half == 1:
                 for w in range(W):
                     j0 = R * ((w + s) % W)
@@ -291,13 +289,16 @@ def tile_matchmatrix_pa_t_w4_kernel(
                 leaky(q, 0)
             if 1 <= q <= last:
                 quantize(q - 1)
+            if q < last:
+                leaky(q, 1)
             if q >= 2:
                 add_bias(q - 2)
             if q < last:
-                for b in range(1, QUAD):
-                    leaky(q, b)
+                leaky(q, 2)
             if q >= 2:
                 finish(q - 2)
+            if q < last:
+                leaky(q, 3)
             if 1 <= q <= last:
                 second_layer(q - 1)
             if q == 0:

@@ -36,6 +36,9 @@ def tile_matchmatrix_pa_t_w4_kernel(
         yps = ctx.enter_context(tc.psum_pool(name="yps", bufs=2))
         ctx.enter_context(tc.manual_schedule())
 
+        probe = keep.tile([P, 1], F32)
+        nc.vector.memset(probe[:], 0.0)
+
         b_raw = keep.tile([P, D], BF16, align_bytes=64)
         nc.sync.dma_start(out=b_raw[:], in_=sent_b.rearrange("n j k -> (n j) k"))
         a_bytes = keep.tile([P, NB, D], U8, align_bytes=64)
@@ -49,6 +52,9 @@ def tile_matchmatrix_pa_t_w4_kernel(
         nc.scalar.dma_start(out=b1_all[:], in_=b1.partition_broadcast(P))
         b2_all = keep.tile([P, K1], BF16)
         nc.scalar.dma_start(out=b2_all[:], in_=b2.partition_broadcast(P))
+
+        warm = keep.tile([P, 1], F32)
+        nc.scalar.activation(out=warm[:], in_=probe[:], func=COPY, scale=SLOPE)
 
         w1_sc = keep.tile([P, 2, K0], U8, align_bytes=64)
         w2_sc = keep.tile([P, K1], U8, align_bytes=64)
@@ -124,19 +130,20 @@ def tile_matchmatrix_pa_t_w4_kernel(
         rep_codes = keep.tile([P, NB, R, Z, W], U32, align_bytes=64)
         rep_scales = keep.tile([P, NB, R, Z, W], U8, align_bytes=64)
 
-        def repeat_b(n):
-            cols = slice(n * NJ, (n + 1) * NJ)
+        def repeat_b(n, r0, r1):
+            cols = slice(n * NJ + r0 * W, n * NJ + r1 * W)
+            nr = r1 - r0
             nc.vector.tensor_copy(
-                out=rep_codes[:, n].rearrange("p r z w -> p (r z w)").bitcast(I32).rearrange("p (r z w) -> p r z w", r=R, z=Z),
-                in_=b_codes[:, cols].bitcast(I32).rearrange("p (r w) -> p r w", r=R).unsqueeze(2).to_broadcast([P, R, Z, W]),
+                out=rep_codes[:, n, r0:r1].rearrange("p r z w -> p (r z w)").bitcast(I32).rearrange("p (r z w) -> p r z w", r=nr, z=Z),
+                in_=b_codes[:, cols].bitcast(I32).rearrange("p (r w) -> p r w", r=nr).unsqueeze(2).to_broadcast([P, nr, Z, W]),
             )
             nc.vector.tensor_copy(
-                out=rep_scales[:, n].rearrange("p r z w -> p (r z w)").bitcast(I32).rearrange("p (r z w) -> p r z w", r=R, z=Z),
+                out=rep_scales[:, n, r0:r1].rearrange("p r z w -> p (r z w)").bitcast(I32).rearrange("p (r z w) -> p r z w", r=nr, z=Z),
                 in_=b_scales[:, cols]
                 .bitcast(I32)
-                .rearrange("p (r w) -> p r w", r=R)
+                .rearrange("p (r w) -> p r w", r=nr)
                 .unsqueeze(2)
-                .to_broadcast([P, R, Z, W // 4]),
+                .to_broadcast([P, nr, Z, W // 4]),
             )
 
         a_part = keep.tile([P, NB, 4, P], F32)
@@ -173,18 +180,19 @@ def tile_matchmatrix_pa_t_w4_kernel(
             )
             dst = b_part[:, n, r]
             view = pb[:].rearrange("q (m t) -> q t m", t=4)
-            if r % 2 == 0:
+            if r % 2 == 0 or (n == 1 and r % 4 == 1):
                 nc.scalar.copy(out=dst, in_=view)
             else:
                 nc.vector.tensor_copy(out=dst, in_=view)
 
         xt_a0 = turn(a_raw0[:])
         grouped0 = group_a(0, xt_a0)
-        repeat_b(0)
+        repeat_b(0, 0, QUAD)
         codes0, scales0 = quantize_a(0, grouped0)
         a_layer(0, codes0, scales0)
         for r in range(QUAD):
             b_layer(0, r)
+        repeat_b(0, QUAD, R)
 
         quads = [(n, s, h) for n in range(NB) for s in range(W) for h in range(2)]
         live = {}
@@ -234,8 +242,8 @@ def tile_matchmatrix_pa_t_w4_kernel(
 
         def quantize(q):
             hidden = live[q][3]
-            codes = work.tile([P, QUAD * P], U32, name="codes", tag="codes", align_bytes=64)
-            scales = work.tile([P, QUAD * P], U8, name="scales", tag="scales", align_bytes=64)
+            codes = work.tile([P, QUAD * P], U32, name="codes", tag="codes", bufs=4, align_bytes=64)
+            scales = work.tile([P, QUAD * P], U8, name="scales", tag="scales", bufs=4, align_bytes=64)
             nc.vector.quantize_mx(
                 out=codes[:].bitcast(FP8X4), scales=scales[:], in_=hidden[:].rearrange("m b c t -> m (b c t)")
             )
@@ -244,6 +252,15 @@ def tile_matchmatrix_pa_t_w4_kernel(
         def second_layer(q):
             codes, scales = live[q]
             y = yps.tile([P, QUAD, K1], F32, name="y", tag="y")
+            nc.tensor.matmul_mx(
+                out=y[:].rearrange("c b k -> c (b k)"),
+                lhsT=codes0[:].bitcast(FP8X4),
+                lhsT_scale=scales0[:],
+                rhs=w1[:, 0, :].bitcast(FP4X4),
+                rhs_scale=w1_sc[:, 0, :],
+                start=True,
+                stop=True,
+            )
             for b in range(QUAD):
                 cols = slice(b * P, (b + 1) * P)
                 nc.tensor.matmul_mx(
@@ -282,25 +299,25 @@ def tile_matchmatrix_pa_t_w4_kernel(
 
         last = len(quads)
         state = {}
-        for q in range(last + 2):
+        for q in range(last + 3):
             if q < last:
                 sums(q)
+            if 2 <= q < last + 2:
+                second_layer(q - 2)
             if q < last:
                 leaky(q, 0)
             if 1 <= q <= last:
                 quantize(q - 1)
             if q < last:
                 leaky(q, 1)
-            if q >= 2:
-                add_bias(q - 2)
+            if q >= 3:
+                add_bias(q - 3)
             if q < last:
                 leaky(q, 2)
-            if q >= 2:
-                finish(q - 2)
+            if q >= 3:
+                finish(q - 3)
             if q < last:
                 leaky(q, 3)
-            if 1 <= q <= last:
-                second_layer(q - 1)
             if q == 0:
                 for r in range(QUAD, R):
                     b_layer(0, r)
@@ -308,7 +325,7 @@ def tile_matchmatrix_pa_t_w4_kernel(
                 state["raw"] = widen(1)
             if q == 4:
                 state["grouped"] = group_a(1, turn(state["raw"][:]))
-                repeat_b(1)
+                repeat_b(1, 0, R)
             if q == 5:
                 state["codes"] = quantize_a(1, state["grouped"])
             if q == 6:

@@ -22,7 +22,7 @@ R = 8
 W = 8
 Z = 16
 QUAD = 4
-TWO_READ = (0, 1)
+LATE = 2
 
 
 def tile_matchmatrix_pa_t_w4_kernel(
@@ -31,43 +31,42 @@ def tile_matchmatrix_pa_t_w4_kernel(
     nc = tc.nc
     with ExitStack() as ctx:
         keep = ctx.enter_context(tc.tile_pool(name="keep", bufs=1))
-        work = ctx.enter_context(tc.tile_pool(name="work", bufs=3))
+        work = ctx.enter_context(tc.tile_pool(name="work", bufs=4))
         xps = ctx.enter_context(tc.psum_pool(name="xps", bufs=6))
         yps = ctx.enter_context(tc.psum_pool(name="yps", bufs=2))
         ctx.enter_context(tc.manual_schedule())
 
-        probe = keep.tile([P, 1], F32)
-        nc.vector.memset(probe[:], 0.0)
-
         b_raw = keep.tile([P, D], BF16, align_bytes=64)
         nc.sync.dma_start(out=b_raw[:], in_=sent_b.rearrange("n j k -> (n j) k"))
+        a_scale = keep.tile([P, 4], F32)
+        nc.scalar.dma_start(out=a_scale[:], in_=sent_a_scale.rearrange("x y (p t) -> p (x y t)", t=4))
         a_bytes = keep.tile([P, NB, D], U8, align_bytes=64)
         nc.sync.dma_start(out=a_bytes[:], in_=sent_a_bytes.rearrange("n i k -> i n k"))
-        a_scale = keep.tile([P, D], F32)
-        nc.scalar.dma_start(out=a_scale[:], in_=sent_a_scale.rearrange("x y k -> (x y k)").partition_broadcast(P))
-        w1 = keep.tile([P, 2, 2 * K0], U8, align_bytes=64)
-        nc.sync.dma_start(out=w1[:, 0, :].bitcast(I32), in_=w1_words[0].bitcast(I32))
-        nc.sync.dma_start(out=w1[:, 1, :].bitcast(I32), in_=w1_words[1].bitcast(I32))
         b1_all = keep.tile([P, K0], BF16)
         nc.scalar.dma_start(out=b1_all[:], in_=b1.partition_broadcast(P))
-        b2_all = keep.tile([P, K1], BF16)
-        nc.scalar.dma_start(out=b2_all[:], in_=b2.partition_broadcast(P))
-
-        warm = keep.tile([P, 1], F32)
-        nc.scalar.activation(out=warm[:], in_=probe[:], func=COPY, scale=SLOPE)
-
+        w1 = keep.tile([P, 2, 2 * K0], U8, align_bytes=64)
         w1_sc = keep.tile([P, 2, K0], U8, align_bytes=64)
+        w2 = keep.tile([P, 2 * K1], U8, align_bytes=64)
         w2_sc = keep.tile([P, K1], U8, align_bytes=64)
         b_scales = keep.tile([P, P], U8, align_bytes=64)
+        probe = keep.tile([P, 1], F32)
+        idle = keep.tile([P, 4 * P], BF16)
+        nc.vector.memset(idle[:], 0.0)
         nc.vector.memset(w1_sc[:].rearrange("p g n -> p (g n)").bitcast(I32), 0)
+        nc.vector.memset(probe[:], 0.0)
         nc.vector.memset(b_scales[:].bitcast(I32), 0)
         nc.vector.memset(w2_sc[:].bitcast(I32), 0)
+        for g in (1, 0):
+            nc.sync.dma_start(out=w1[:, g, :].bitcast(I32), in_=w1_words[g].bitcast(I32))
         for q in range(4):
             nc.sync.dma_start(
                 out=w1_sc[32 * q : 32 * q + 4, :, :].bitcast(I32),
                 in_=w1_scales[:, 4 * q : 4 * q + 4, :].rearrange("g q n -> q g n").bitcast(I32),
             )
-        w2 = keep.tile([P, 2 * K1], U8, align_bytes=64)
+        warm = keep.tile([P, 1], F32)
+        nc.scalar.activation(out=warm[:], in_=probe[:], func=COPY, scale=SLOPE)
+        b2_all = keep.tile([P, K1], BF16)
+        nc.sync.dma_start(out=b2_all[:], in_=b2.partition_broadcast(P))
         nc.sync.dma_start(out=w2[:].bitcast(I32), in_=w2_words[0].bitcast(I32))
         for q in range(4):
             nc.sync.dma_start(
@@ -92,41 +91,11 @@ def tile_matchmatrix_pa_t_w4_kernel(
 
         def widen(n):
             a_raw = keep.tile([P, D], BF16, align_bytes=64, name=f"a_raw{n}")
-            nc.vector.tensor_tensor(out=a_raw[:], in0=a_bytes[:, n, :].bitcast(FP8), in1=a_scale[:], op=ALU.mult)
+            nc.scalar.copy(out=a_raw[:], in_=a_bytes[:, n, :].bitcast(FP8))
             return a_raw
 
         b_grouped = keep.tile([P, P, 4], BF16, align_bytes=64)
         b_codes = keep.tile([P, P], U32, align_bytes=64)
-        xt_b = turn(b_raw[:])
-        a_raw0 = widen(0)
-        for n in range(NB):
-            nc.vector.tensor_copy(
-                out=b_grouped[:, n * NJ : (n + 1) * NJ, :]
-                .rearrange("p c t -> p (c t)")
-                .bitcast(F32)
-                .rearrange("p (r w u) -> p r w u", r=R, w=W),
-                in_=xt_b[:, :, n * NJ : (n + 1) * NJ].rearrange("p u (w r) -> p r w u", r=R),
-            )
-        nc.vector.quantize_mx(
-            out=b_codes[:].bitcast(FP8X4), scales=b_scales[:], in_=b_grouped[:].rearrange("p c t -> p (c t)")
-        )
-
-        def group_a(n, xt):
-            a_grouped = keep.tile([P, P, 4], BF16, align_bytes=64, name=f"a_grouped{n}")
-            nc.scalar.copy(
-                out=a_grouped[:].rearrange("p c t -> p (c t)").bitcast(F32).rearrange("p (c u) -> p c u", u=2),
-                in_=xt[:].rearrange("p u c -> p c u"),
-            )
-            return a_grouped
-
-        def quantize_a(n, a_grouped):
-            a_codes = keep.tile([P, P], U32, align_bytes=64, name=f"a_codes{n}")
-            a_scales = keep.tile([P, P], U8, align_bytes=64, name=f"a_scales{n}")
-            nc.vector.quantize_mx(
-                out=a_codes[:].bitcast(FP8X4), scales=a_scales[:], in_=a_grouped[:].rearrange("p c t -> p (c t)")
-            )
-            return a_codes, a_scales
-
         rep_codes = keep.tile([P, NB, R, Z, W], U32, align_bytes=64)
         rep_scales = keep.tile([P, NB, R, Z, W], U8, align_bytes=64)
 
@@ -145,6 +114,29 @@ def tile_matchmatrix_pa_t_w4_kernel(
                 .unsqueeze(2)
                 .to_broadcast([P, nr, Z, W // 4]),
             )
+
+        def group_a(n, xt):
+            a_mixed = keep.tile([P, P, 4], BF16, align_bytes=64, name=f"a_mixed{n}")
+            nc.scalar.copy(
+                out=a_mixed[:].rearrange("p c t -> p (c t)").bitcast(F32).rearrange("p (c u) -> p c u", u=2),
+                in_=xt[:].rearrange("p u c -> p c u"),
+            )
+            return a_mixed
+
+        def scale_a(n, a_mixed):
+            a_grouped = keep.tile([P, P, 4], BF16, align_bytes=64, name=f"a_grouped{n}")
+            nc.vector.tensor_tensor(
+                out=a_grouped[:], in0=a_mixed[:], in1=a_scale[:].unsqueeze(1).to_broadcast([P, P, 4]), op=ALU.mult
+            )
+            return a_grouped
+
+        def quantize_a(n, a_grouped):
+            a_codes = keep.tile([P, P], U32, align_bytes=64, name=f"a_codes{n}")
+            a_scales = keep.tile([P, P], U8, align_bytes=64, name=f"a_scales{n}")
+            nc.vector.quantize_mx(
+                out=a_codes[:].bitcast(FP8X4), scales=a_scales[:], in_=a_grouped[:].rearrange("p c t -> p (c t)")
+            )
+            return a_codes, a_scales
 
         a_part = keep.tile([P, NB, 4, P], F32)
         b_part = keep.tile([P, NB, R, 4, P], F32)
@@ -167,7 +159,7 @@ def tile_matchmatrix_pa_t_w4_kernel(
                 op=ALU.add,
             )
 
-        def b_layer(n, r):
+        def b_layer(n, r, scalar):
             pb = xps.tile([P, K0], F32, name="pb", tag="x")
             nc.tensor.matmul_mx(
                 out=pb[:],
@@ -180,70 +172,130 @@ def tile_matchmatrix_pa_t_w4_kernel(
             )
             dst = b_part[:, n, r]
             view = pb[:].rearrange("q (m t) -> q t m", t=4)
-            if r % 2 == 0 or (n == 1 and r % 4 == 1):
+            if scalar:
                 nc.scalar.copy(out=dst, in_=view)
             else:
                 nc.vector.tensor_copy(out=dst, in_=view)
 
+        def park_b():
+            pb = xps.tile([P, K0], F32, name="pb", tag="x")
+            nc.tensor.matmul_mx(
+                out=pb[:],
+                lhsT=b_codes[:].bitcast(FP8X4),
+                lhsT_scale=b_scales[:],
+                rhs=w1[:, 1, :].bitcast(FP4X4),
+                rhs_scale=w1_sc[:, 1, :],
+                start=True,
+                stop=True,
+            )
+            b_rows = keep.tile([P, 4, P], F32)
+            nc.scalar.copy(out=b_rows[:], in_=pb[:].rearrange("q (m t) -> q t m", t=4))
+            park = out[1, 120:124].rearrange("i j k -> (i j k)")
+            nc.sync.dma_start(
+                out=park.rearrange("(j c) -> j c", c=K0), in_=b_rows[NJ:, :, :].rearrange("j t m -> j (t m)")
+            )
+            rows = park.rearrange("(r w c) -> w r c", r=R, w=W)
+            for w in range(W):
+                nc.sync.dma_start(
+                    out=b_part[w::W, 1].rearrange("q r t m -> q r (t m)"), in_=rows[w].partition_broadcast(Z)
+                )
+
+        spin = yps.tile([P, 4 * P], F32, name="spin", tag="y")
+
+        def turn_over(times):
+            for i in range(times):
+                nc.tensor.matmul(spin[:], lhsT=idle[:, :P], rhs=idle[:], start=True, stop=True)
+
+        def group_b(n):
+            half = slice(n * NJ, (n + 1) * NJ)
+            nc.vector.tensor_copy(
+                out=b_grouped[:, half, :]
+                .rearrange("p c t -> p (c t)")
+                .bitcast(F32)
+                .rearrange("p (r w u) -> p r w u", r=R, w=W),
+                in_=xt_b[:, :, half].rearrange("p u (w r) -> p r w u", r=R),
+            )
+
+        def quantize_b(n):
+            half = slice(n * NJ, (n + 1) * NJ)
+            nc.vector.quantize_mx(
+                out=b_codes[:, half].bitcast(FP8X4),
+                scales=b_scales[:, half],
+                in_=b_grouped[:, half, :].rearrange("p c t -> p (c t)"),
+            )
+
+        turn_over(3)
+        xt_b = turn(b_raw[:])
+        turn_over(2)
+        a_raw0 = widen(0)
         xt_a0 = turn(a_raw0[:])
-        grouped0 = group_a(0, xt_a0)
+        turn_over(1)
+        group_b(0)
+        group_b(1)
+        quantize_b(0)
+        mixed0 = group_a(0, xt_a0)
         repeat_b(0, 0, QUAD)
-        codes0, scales0 = quantize_a(0, grouped0)
-        a_layer(0, codes0, scales0)
-        for r in range(QUAD):
-            b_layer(0, r)
+        grouped0 = scale_a(0, mixed0)
         repeat_b(0, QUAD, R)
+        codes0, scales0 = quantize_a(0, grouped0)
+        quantize_b(1)
+        b_layer(0, 0, True)
+        b_layer(0, 1, True)
+        a_layer(0, codes0, scales0)
+        b_layer(0, 2, True)
+        b_layer(0, 3, True)
 
         quads = [(n, s, h) for n in range(NB) for s in range(W) for h in range(2)]
+        last = len(quads)
         live = {}
-        outs = {}
+        groups = {}
 
-        def sums(q):
+        def one_read(q):
+            return 1 if q >= last - LATE else 2
+
+        def sums(q, b):
             n, s, half = quads[q]
+            single = one_read(q)
+            if b == 0:
+                live[q] = {
+                    "pair": work.tile([P, QUAD - single, P, 4], BF16, name="pair", tag="pair"),
+                    "small": work.tile([P, QUAD - single, P, 4], BF16, name="small", tag="small"),
+                    "hidden": work.tile([P, QUAD, P, 4], BF16, name="hidden", tag="hidden", align_bytes=64),
+                }
             picks = shifts[:].rearrange("q w z -> q (w z)")[:, s * Z : s * Z + P]
-            firsts = []
-            seconds = []
-            xs = []
-            for b in range(QUAD):
-                r = half * QUAD + b
-                x = xps.tile([P, 4, P], F32, name="x", tag="x")
-                for t in range(4):
-                    nc.tensor.matmul(
-                        x[:, t, :], lhsT=a_part[:, n, t, :], rhs=ident[:], is_transpose=True, start=True, stop=False
-                    )
-                    nc.tensor.matmul(
-                        x[:, t, :], lhsT=b_part[:, n, r, t, :], rhs=picks, is_transpose=True, start=False, stop=True
-                    )
-                first = work.tile([P, P, 4], BF16, name="first", tag="first", bufs=6)
-                nc.scalar.copy(out=first[:], in_=x[:].rearrange("m t c -> m c t"))
-                second = None
-                if b in TWO_READ:
-                    second = work.tile([P, P, 4], BF16, name="second", tag="second", bufs=4)
-                    nc.scalar.activation(out=second[:], in_=x[:].rearrange("m t c -> m c t"), func=COPY, scale=SLOPE)
-                xs.append(x)
-                firsts.append(first)
-                seconds.append(second)
-            hidden = work.tile([P, QUAD, P, 4], BF16, name="hidden", tag="hidden", align_bytes=64)
-            live[q] = (xs, firsts, seconds, hidden)
+            r = half * QUAD + b
+            x = xps.tile([P, 4, P], F32, name="x", tag="x")
+            for t in range(4):
+                nc.tensor.matmul(
+                    x[:, t, :], lhsT=a_part[:, n, t, :], rhs=ident[:], is_transpose=True, start=True, stop=False
+                )
+                nc.tensor.matmul(
+                    x[:, t, :], lhsT=b_part[:, n, r, t, :], rhs=picks, is_transpose=True, start=False, stop=True
+                )
+            view = x[:].rearrange("m t c -> m c t")
+            if b < single:
+                first = work.tile([P, P, 4], BF16, name="first", tag="first", bufs=8)
+                nc.scalar.copy(out=first[:], in_=view)
+                live[q][b] = (view, first)
+            else:
+                nc.scalar.copy(out=live[q]["pair"][:, b - single], in_=view)
+                nc.scalar.activation(out=live[q]["small"][:, b - single], in_=view, func=COPY, scale=SLOPE)
 
         def leaky(q, b):
-            xs, firsts, seconds, hidden = live[q]
-            if seconds[b] is None:
-                nc.vector.scalar_tensor_tensor(
-                    out=hidden[:, b],
-                    in0=xs[b][:].rearrange("m t c -> m c t"),
-                    scalar=SLOPE,
-                    in1=firsts[b][:],
-                    op0=ALU.mult,
-                    op1=ALU.max,
-                )
-            else:
-                nc.vector.tensor_tensor(out=hidden[:, b], in0=firsts[b][:], in1=seconds[b][:], op=ALU.max)
+            view, first = live[q][b]
+            nc.vector.scalar_tensor_tensor(
+                out=live[q]["hidden"][:, b], in0=view, scalar=SLOPE, in1=first[:], op0=ALU.mult, op1=ALU.max
+            )
+
+        def leaky_pair(q):
+            nc.vector.tensor_tensor(
+                out=live[q]["hidden"][:, one_read(q) :], in0=live[q]["pair"][:], in1=live[q]["small"][:], op=ALU.max
+            )
 
         def quantize(q):
-            hidden = live[q][3]
-            codes = work.tile([P, QUAD * P], U32, name="codes", tag="codes", bufs=4, align_bytes=64)
-            scales = work.tile([P, QUAD * P], U8, name="scales", tag="scales", bufs=4, align_bytes=64)
+            hidden = live[q]["hidden"]
+            codes = work.tile([P, QUAD * P], U32, name="codes", tag="codes", align_bytes=64)
+            scales = work.tile([P, QUAD * P], U8, name="scales", tag="scales", align_bytes=64)
             nc.vector.quantize_mx(
                 out=codes[:].bitcast(FP8X4), scales=scales[:], in_=hidden[:].rearrange("m b c t -> m (b c t)")
             )
@@ -252,15 +304,6 @@ def tile_matchmatrix_pa_t_w4_kernel(
         def second_layer(q):
             codes, scales = live[q]
             y = yps.tile([P, QUAD, K1], F32, name="y", tag="y")
-            nc.tensor.matmul_mx(
-                out=y[:].rearrange("c b k -> c (b k)"),
-                lhsT=codes0[:].bitcast(FP8X4),
-                lhsT_scale=scales0[:],
-                rhs=w1[:, 0, :].bitcast(FP4X4),
-                rhs_scale=w1_sc[:, 0, :],
-                start=True,
-                stop=True,
-            )
             for b in range(QUAD):
                 cols = slice(b * P, (b + 1) * P)
                 nc.tensor.matmul_mx(
@@ -275,60 +318,74 @@ def tile_matchmatrix_pa_t_w4_kernel(
             live[q] = y
 
         def add_bias(q):
-            y = live[q]
-            z = work.tile([P, QUAD, K1], F32, name="z", tag="z")
+            y = live.pop(q)
+            if q % 2 == 0:
+                groups[q // 2] = (
+                    work.tile([P, R, K1], F32, name="z", tag="z", bufs=3),
+                    work.tile([P, R, K1], F32, name="o", tag="o", bufs=16),
+                )
+            z = groups[q // 2][0]
+            half = slice((q % 2) * QUAD, (q % 2 + 1) * QUAD)
             nc.vector.tensor_tensor(
-                out=z[:], in0=y[:], in1=b2_all[:].unsqueeze(1).to_broadcast([P, QUAD, K1]), op=ALU.add
+                out=z[:, half, :], in0=y[:], in1=b2_all[:].unsqueeze(1).to_broadcast([P, QUAD, K1]), op=ALU.add
             )
-            live[q] = z
 
-        def finish(q):
-            n, s, half = quads[q]
-            z = live.pop(q)
-            if half == 0:
-                outs[q // 2] = work.tile([P, R, K1], F32, name="o", tag="o")
-            o = outs[q // 2]
+        def finish(g, r0, r1):
+            n, s = divmod(g, W)
+            z, o = groups[g]
             nc.vector.scalar_tensor_tensor(
-                out=o[:, half * QUAD : (half + 1) * QUAD, :], in0=z[:], scalar=SLOPE, in1=z[:], op0=ALU.mult, op1=ALU.max
+                out=o[:, r0:r1, :], in0=z[:, r0:r1, :], scalar=SLOPE, in1=z[:, r0:r1, :], op0=ALU.mult, op1=ALU.max
             )
-            if half == 1:
-                for w in range(W):
-                    j0 = R * ((w + s) % W)
-                    rows = slice(Z * w, Z * (w + 1))
-                    nc.sync.dma_start(out=out[n, rows, j0 : j0 + R, :], in_=o[rows, :, :])
+            for w in range(W):
+                j0 = R * ((w + s) % W)
+                rows = slice(Z * w, Z * (w + 1))
+                nc.sync.dma_start(out=out[n, rows, j0 + r0 : j0 + r1, :], in_=o[rows, r0:r1, :])
 
-        last = len(quads)
         state = {}
-        for q in range(last + 3):
+        for q in range(last + 4):
+            if q == 0:
+                sums(0, 0)
+                sums(0, 1)
+                b_layer(0, 4, False)
+                b_layer(0, 5, False)
+                leaky(0, 0)
+                sums(0, 2)
+                b_layer(0, 6, False)
+                leaky(0, 1)
+                sums(0, 3)
+                b_layer(0, 7, False)
+                leaky_pair(0)
+                continue
             if q < last:
-                sums(q)
+                for b in range(QUAD):
+                    sums(q, b)
             if 2 <= q < last + 2:
                 second_layer(q - 2)
             if q < last:
                 leaky(q, 0)
             if 1 <= q <= last:
                 quantize(q - 1)
-            if q < last:
+            if q < last and one_read(q) == 2:
                 leaky(q, 1)
-            if q >= 3:
+            if q >= 5 and q % 2 == 1 and q - 4 < last - 2:
+                finish((q - 4) // 2, 0, R)
+            if q == last + 2:
+                finish(last // 2 - 1, 0, QUAD)
+            if 3 <= q < last + 3:
                 add_bias(q - 3)
+            if q == last + 3:
+                finish(last // 2 - 1, QUAD, R)
             if q < last:
-                leaky(q, 2)
-            if q >= 3:
-                finish(q - 3)
-            if q < last:
-                leaky(q, 3)
-            if q == 0:
-                for r in range(QUAD, R):
-                    b_layer(0, r)
+                leaky_pair(q)
+            if q == 2:
+                park_b()
             if q == 3:
                 state["raw"] = widen(1)
             if q == 4:
-                state["grouped"] = group_a(1, turn(state["raw"][:]))
-                repeat_b(1, 0, R)
+                state["mixed"] = group_a(1, turn(state["raw"][:]))
             if q == 5:
-                state["codes"] = quantize_a(1, state["grouped"])
+                state["grouped"] = scale_a(1, state["mixed"])
             if q == 6:
+                state["codes"] = quantize_a(1, state["grouped"])
+            if q == 7:
                 a_layer(1, state["codes"][0], state["codes"][1])
-            if 7 <= q < 7 + R:
-                b_layer(1, q - 7)

from contextlib import ExitStack

import concourse.mybir as mybir
from concourse.masks import make_identity

F32 = mybir.dt.float32
BF16 = mybir.dt.bfloat16
I32 = mybir.dt.int32
U32 = mybir.dt.uint32
U8 = mybir.dt.uint8
FP8 = mybir.dt.float8_e4m3fn
FP8X4 = mybir.dt.float8_e4m3fn_x4
FP4X4 = mybir.dt.float4_e2m1fn_x4
ALU = mybir.AluOpType
COPY = mybir.ActivationFunctionType.Copy

P = 128
NB, NI, NJ, D, K0, K1 = 2, 128, 64, 512, 512, 128
FLOPS = 2 * (NB * (NI + NJ) * D * K0 + NB * NI * NJ * K0 * K1)
SLOPE = 0.01
R = 8
W = 8
Z = 16
QUAD = 4
LATE = 2


def tile_matchmatrix_pa_t_w4_kernel(
    tc, sent_a_bytes, sent_a_scale, sent_b, w1_words, w1_scales, b1, w2_words, w2_scales, b2, out
):
    nc = tc.nc
    with ExitStack() as ctx:
        keep = ctx.enter_context(tc.tile_pool(name="keep", bufs=1))
        work = ctx.enter_context(tc.tile_pool(name="work", bufs=4))
        xps = ctx.enter_context(tc.psum_pool(name="xps", bufs=6))
        yps = ctx.enter_context(tc.psum_pool(name="yps", bufs=2))
        ctx.enter_context(tc.manual_schedule())

        b_raw = keep.tile([P, D], BF16, align_bytes=64)
        nc.sync.dma_start(out=b_raw[:], in_=sent_b.rearrange("n j k -> (n j) k"))
        a_scale = keep.tile([P, 4], F32)
        nc.scalar.dma_start(out=a_scale[:], in_=sent_a_scale.rearrange("x y (p t) -> p (x y t)", t=4))
        a_bytes = keep.tile([P, NB, D], U8, align_bytes=64)
        nc.sync.dma_start(out=a_bytes[:], in_=sent_a_bytes.rearrange("n i k -> i n k"))
        b1_all = keep.tile([P, K0], BF16)
        nc.scalar.dma_start(out=b1_all[:], in_=b1.partition_broadcast(P))
        w1 = keep.tile([P, 2, 2 * K0], U8, align_bytes=64)
        w1_sc = keep.tile([P, 2, K0], U8, align_bytes=64)
        w2 = keep.tile([P, 2 * K1], U8, align_bytes=64)
        w2_sc = keep.tile([P, K1], U8, align_bytes=64)
        b_scales = keep.tile([P, P], U8, align_bytes=64)
        probe = keep.tile([P, 1], F32)
        idle = keep.tile([P, 4 * P], BF16)
        nc.vector.memset(idle[:], 0.0)
        nc.vector.memset(w1_sc[:].rearrange("p g n -> p (g n)").bitcast(I32), 0)
        nc.vector.memset(probe[:], 0.0)
        nc.vector.memset(b_scales[:].bitcast(I32), 0)
        nc.vector.memset(w2_sc[:].bitcast(I32), 0)
        for g in (1, 0):
            nc.sync.dma_start(out=w1[:, g, :].bitcast(I32), in_=w1_words[g].bitcast(I32))
        for q in range(4):
            nc.sync.dma_start(
                out=w1_sc[32 * q : 32 * q + 4, :, :].bitcast(I32),
                in_=w1_scales[:, 4 * q : 4 * q + 4, :].rearrange("g q n -> q g n").bitcast(I32),
            )
        warm = keep.tile([P, 1], F32)
        nc.scalar.activation(out=warm[:], in_=probe[:], func=COPY, scale=SLOPE)
        b2_all = keep.tile([P, K1], BF16)
        nc.sync.dma_start(out=b2_all[:], in_=b2.partition_broadcast(P))
        nc.sync.dma_start(out=w2[:].bitcast(I32), in_=w2_words[0].bitcast(I32))
        for q in range(4):
            nc.sync.dma_start(
                out=w2_sc[32 * q : 32 * q + 4, :].bitcast(I32),
                in_=w2_scales[0, 4 * q : 4 * q + 4, :].bitcast(I32),
            )

        ident = keep.tile([P, P], F32)
        make_identity(nc, ident[:])
        shifts = keep.tile([P, 2 * W, Z], F32)
        for half in range(2):
            nc.vector.tensor_copy(
                out=shifts[:, half * W : (half + 1) * W, :], in_=ident[:].rearrange("q (z w) -> q w z", w=W)
            )

        def turn(raw):
            words = raw.bitcast(F32)
            xt = xps.tile([P, 2, P], F32, name="xt", tag="x")
            for u in range(2):
                nc.tensor.transpose(xt[:, u, :], words[:, u : 2 * P : 2], ident[:])
            return xt

        def widen(n):
            a_raw = keep.tile([P, D], BF16, align_bytes=64, name=f"a_raw{n}")
            nc.scalar.copy(out=a_raw[:], in_=a_bytes[:, n, :].bitcast(FP8))
            return a_raw

        b_grouped = keep.tile([P, P, 4], BF16, align_bytes=64)
        b_codes = keep.tile([P, P], U32, align_bytes=64)
        rep_codes = keep.tile([P, NB, R, Z, W], U32, align_bytes=64)
        rep_scales = keep.tile([P, NB, R, Z, W], U8, align_bytes=64)

        def repeat_b(n, r0, r1):
            cols = slice(n * NJ + r0 * W, n * NJ + r1 * W)
            nr = r1 - r0
            nc.vector.tensor_copy(
                out=rep_codes[:, n, r0:r1].rearrange("p r z w -> p (r z w)").bitcast(I32).rearrange("p (r z w) -> p r z w", r=nr, z=Z),
                in_=b_codes[:, cols].bitcast(I32).rearrange("p (r w) -> p r w", r=nr).unsqueeze(2).to_broadcast([P, nr, Z, W]),
            )
            nc.vector.tensor_copy(
                out=rep_scales[:, n, r0:r1].rearrange("p r z w -> p (r z w)").bitcast(I32).rearrange("p (r z w) -> p r z w", r=nr, z=Z),
                in_=b_scales[:, cols]
                .bitcast(I32)
                .rearrange("p (r w) -> p r w", r=nr)
                .unsqueeze(2)
                .to_broadcast([P, nr, Z, W // 4]),
            )

        def group_a(n, xt):
            a_mixed = keep.tile([P, P, 4], BF16, align_bytes=64, name=f"a_mixed{n}")
            nc.scalar.copy(
                out=a_mixed[:].rearrange("p c t -> p (c t)").bitcast(F32).rearrange("p (c u) -> p c u", u=2),
                in_=xt[:].rearrange("p u c -> p c u"),
            )
            return a_mixed

        def scale_a(n, a_mixed):
            a_grouped = keep.tile([P, P, 4], BF16, align_bytes=64, name=f"a_grouped{n}")
            nc.vector.tensor_tensor(
                out=a_grouped[:], in0=a_mixed[:], in1=a_scale[:].unsqueeze(1).to_broadcast([P, P, 4]), op=ALU.mult
            )
            return a_grouped

        def quantize_a(n, a_grouped):
            a_codes = keep.tile([P, P], U32, align_bytes=64, name=f"a_codes{n}")
            a_scales = keep.tile([P, P], U8, align_bytes=64, name=f"a_scales{n}")
            nc.vector.quantize_mx(
                out=a_codes[:].bitcast(FP8X4), scales=a_scales[:], in_=a_grouped[:].rearrange("p c t -> p (c t)")
            )
            return a_codes, a_scales

        a_part = keep.tile([P, NB, 4, P], F32)
        b_part = keep.tile([P, NB, R, 4, P], F32)

        def a_layer(n, a_codes, a_scales):
            pa = xps.tile([P, K0], F32, name="pa", tag="x")
            nc.tensor.matmul_mx(
                out=pa[:],
                lhsT=a_codes[:].bitcast(FP8X4),
                lhsT_scale=a_scales[:],
                rhs=w1[:, 0, :].bitcast(FP4X4),
                rhs_scale=w1_sc[:, 0, :],
                start=True,
                stop=True,
            )
            nc.vector.tensor_tensor(
                out=a_part[:, n],
                in0=pa[:].rearrange("i (m t) -> i t m", t=4),
                in1=b1_all[:].rearrange("i (m t) -> i t m", t=4),
                op=ALU.add,
            )

        def b_layer(n, r, scalar):
            pb = xps.tile([P, K0], F32, name="pb", tag="x")
            nc.tensor.matmul_mx(
                out=pb[:],
                lhsT=rep_codes[:, n, r].rearrange("p z w -> p (z w)").bitcast(FP8X4),
                lhsT_scale=rep_scales[:, n, r].rearrange("p z w -> p (z w)"),
                rhs=w1[:, 1, :].bitcast(FP4X4),
                rhs_scale=w1_sc[:, 1, :],
                start=True,
                stop=True,
            )
            dst = b_part[:, n, r]
            view = pb[:].rearrange("q (m t) -> q t m", t=4)
            if scalar:
                nc.scalar.copy(out=dst, in_=view)
            else:
                nc.vector.tensor_copy(out=dst, in_=view)

        def park_b():
            pb = xps.tile([P, K0], F32, name="pb", tag="x")
            nc.tensor.matmul_mx(
                out=pb[:],
                lhsT=b_codes[:].bitcast(FP8X4),
                lhsT_scale=b_scales[:],
                rhs=w1[:, 1, :].bitcast(FP4X4),
                rhs_scale=w1_sc[:, 1, :],
                start=True,
                stop=True,
            )
            b_rows = keep.tile([P, 4, P], F32)
            nc.scalar.copy(out=b_rows[:], in_=pb[:].rearrange("q (m t) -> q t m", t=4))
            park = out[1, 120:124].rearrange("i j k -> (i j k)")
            nc.sync.dma_start(
                out=park.rearrange("(j c) -> j c", c=K0), in_=b_rows[NJ:, :, :].rearrange("j t m -> j (t m)")
            )
            rows = park.rearrange("(r w c) -> w r c", r=R, w=W)
            for w in range(W):
                nc.sync.dma_start(
                    out=b_part[w::W, 1].rearrange("q r t m -> q r (t m)"), in_=rows[w].partition_broadcast(Z)
                )

        spin = yps.tile([P, 4 * P], F32, name="spin", tag="y")

        def turn_over(times):
            for i in range(times):
                nc.tensor.matmul(spin[:], lhsT=idle[:, :P], rhs=idle[:], start=True, stop=True)

        def group_b(n):
            half = slice(n * NJ, (n + 1) * NJ)
            nc.vector.tensor_copy(
                out=b_grouped[:, half, :]
                .rearrange("p c t -> p (c t)")
                .bitcast(F32)
                .rearrange("p (r w u) -> p r w u", r=R, w=W),
                in_=xt_b[:, :, half].rearrange("p u (w r) -> p r w u", r=R),
            )

        def quantize_b(n):
            half = slice(n * NJ, (n + 1) * NJ)
            nc.vector.quantize_mx(
                out=b_codes[:, half].bitcast(FP8X4),
                scales=b_scales[:, half],
                in_=b_grouped[:, half, :].rearrange("p c t -> p (c t)"),
            )

        turn_over(3)
        xt_b = turn(b_raw[:])
        turn_over(2)
        a_raw0 = widen(0)
        xt_a0 = turn(a_raw0[:])
        turn_over(1)
        group_b(0)
        group_b(1)
        quantize_b(0)
        mixed0 = group_a(0, xt_a0)
        repeat_b(0, 0, QUAD)
        grouped0 = scale_a(0, mixed0)
        repeat_b(0, QUAD, R)
        codes0, scales0 = quantize_a(0, grouped0)
        quantize_b(1)
        b_layer(0, 0, True)
        b_layer(0, 1, True)
        a_layer(0, codes0, scales0)
        b_layer(0, 2, True)
        b_layer(0, 3, True)

        quads = [(n, s, h) for n in range(NB) for s in range(W) for h in range(2)]
        last = len(quads)
        live = {}
        groups = {}

        def one_read(q):
            return 1 if q >= last - LATE else 2

        def sums(q, b):
            n, s, half = quads[q]
            single = one_read(q)
            if b == 0:
                live[q] = {
                    "pair": work.tile([P, QUAD - single, P, 4], BF16, name="pair", tag="pair"),
                    "small": work.tile([P, QUAD - single, P, 4], BF16, name="small", tag="small"),
                    "hidden": work.tile([P, QUAD, P, 4], BF16, name="hidden", tag="hidden", align_bytes=64),
                }
            picks = shifts[:].rearrange("q w z -> q (w z)")[:, s * Z : s * Z + P]
            r = half * QUAD + b
            x = xps.tile([P, 4, P], F32, name="x", tag="x")
            for t in range(4):
                nc.tensor.matmul(
                    x[:, t, :], lhsT=a_part[:, n, t, :], rhs=ident[:], is_transpose=True, start=True, stop=False
                )
                nc.tensor.matmul(
                    x[:, t, :], lhsT=b_part[:, n, r, t, :], rhs=picks, is_transpose=True, start=False, stop=True
                )
            view = x[:].rearrange("m t c -> m c t")
            if b < single:
                first = work.tile([P, P, 4], BF16, name="first", tag="first", bufs=8)
                nc.scalar.copy(out=first[:], in_=view)
                live[q][b] = (view, first)
            else:
                nc.scalar.copy(out=live[q]["pair"][:, b - single], in_=view)
                nc.scalar.activation(out=live[q]["small"][:, b - single], in_=view, func=COPY, scale=SLOPE)

        def leaky(q, b):
            view, first = live[q][b]
            nc.vector.scalar_tensor_tensor(
                out=live[q]["hidden"][:, b], in0=view, scalar=SLOPE, in1=first[:], op0=ALU.mult, op1=ALU.max
            )

        def leaky_pair(q):
            nc.vector.tensor_tensor(
                out=live[q]["hidden"][:, one_read(q) :], in0=live[q]["pair"][:], in1=live[q]["small"][:], op=ALU.max
            )

        def quantize(q):
            hidden = live[q]["hidden"]
            codes = work.tile([P, QUAD * P], U32, name="codes", tag="codes", align_bytes=64)
            scales = work.tile([P, QUAD * P], U8, name="scales", tag="scales", align_bytes=64)
            nc.vector.quantize_mx(
                out=codes[:].bitcast(FP8X4), scales=scales[:], in_=hidden[:].rearrange("m b c t -> m (b c t)")
            )
            live[q] = (codes, scales)

        def second_layer(q):
            codes, scales = live[q]
            y = yps.tile([P, QUAD, K1], F32, name="y", tag="y")
            for b in range(QUAD):
                cols = slice(b * P, (b + 1) * P)
                nc.tensor.matmul_mx(
                    out=y[:, b, :],
                    lhsT=codes[:, cols].bitcast(FP8X4),
                    lhsT_scale=scales[:, cols],
                    rhs=w2[:].bitcast(FP4X4),
                    rhs_scale=w2_sc[:],
                    start=True,
                    stop=True,
                )
            live[q] = y

        def add_bias(q):
            y = live.pop(q)
            if q % 2 == 0:
                groups[q // 2] = (
                    work.tile([P, R, K1], F32, name="z", tag="z", bufs=3),
                    work.tile([P, R, K1], F32, name="o", tag="o", bufs=16),
                )
            z = groups[q // 2][0]
            half = slice((q % 2) * QUAD, (q % 2 + 1) * QUAD)
            nc.vector.tensor_tensor(
                out=z[:, half, :], in0=y[:], in1=b2_all[:].unsqueeze(1).to_broadcast([P, QUAD, K1]), op=ALU.add
            )

        def finish(g, r0, r1):
            n, s = divmod(g, W)
            z, o = groups[g]
            nc.vector.scalar_tensor_tensor(
                out=o[:, r0:r1, :], in0=z[:, r0:r1, :], scalar=SLOPE, in1=z[:, r0:r1, :], op0=ALU.mult, op1=ALU.max
            )
            for w in range(W):
                j0 = R * ((w + s) % W)
                rows = slice(Z * w, Z * (w + 1))
                nc.sync.dma_start(out=out[n, rows, j0 + r0 : j0 + r1, :], in_=o[rows, r0:r1, :])

        state = {}
        for q in range(last + 4):
            if q == 0:
                sums(0, 0)
                sums(0, 1)
                b_layer(0, 4, False)
                b_layer(0, 5, False)
                leaky(0, 0)
                sums(0, 2)
                b_layer(0, 6, False)
                leaky(0, 1)
                sums(0, 3)
                b_layer(0, 7, False)
                leaky_pair(0)
                continue
            if q < last:
                for b in range(QUAD):
                    sums(q, b)
            if 2 <= q < last + 2:
                second_layer(q - 2)
            if q < last:
                leaky(q, 0)
            if 1 <= q <= last:
                quantize(q - 1)
            if q < last and one_read(q) == 2:
                leaky(q, 1)
            if q >= 5 and q % 2 == 1 and q - 4 < last - 2:
                finish((q - 4) // 2, 0, R)
            if q == last + 2:
                finish(last // 2 - 1, 0, QUAD)
            if 3 <= q < last + 3:
                add_bias(q - 3)
            if q == last + 3:
                finish(last // 2 - 1, QUAD, R)
            if q < last:
                leaky_pair(q)
            if q == 2:
                park_b()
            if q == 3:
                state["raw"] = widen(1)
            if q == 4:
                state["mixed"] = group_a(1, turn(state["raw"][:]))
            if q == 5:
                state["grouped"] = scale_a(1, state["mixed"])
            if q == 6:
                state["codes"] = quantize_a(1, state["grouped"])
            if q == 7:
                a_layer(1, state["codes"][0], state["codes"][1])
